import numpy as np
import ml_dtypes


def mxq(x, axis, fmt="e4m3"):
    dtype, down = {"e4m3": (ml_dtypes.float8_e4m3fn, 7), "e5m2": (ml_dtypes.float8_e5m2, 14)}[fmt]
    v = np.moveaxis(np.asarray(x, np.float32).astype(ml_dtypes.bfloat16).astype(np.float64), axis, -1)
    blocks = v.reshape(v.shape[:-1] + (-1, 32))
    amax = np.abs(blocks).max(-1, keepdims=True)
    byte = np.maximum(np.where(amax > 0, np.frexp(amax)[1] - 1 + 127, 0) - down, 1)
    scale = np.exp2(byte - 127.0)
    codes = (blocks / scale).astype(np.float32).astype(dtype).astype(np.float64)
    return np.moveaxis((codes * scale).reshape(v.shape), -1, axis)


WIDE = False


def mx_kscale(k):
    if not WIDE:
        return np.ones(k)
    levels = np.array([10, -10, 5, -5, 0])
    a = np.random.permutation(np.resize(levels, k // 512 * 4)).reshape(k // 512, 4)
    idx = np.arange(k)
    return np.exp2(a[idx // 512, idx % 128 // 32])


BF16 = ml_dtypes.bfloat16


def bf(x):
    return np.asarray(x, np.float32).astype(BF16)


def f64(x):
    return np.asarray(x).astype(np.float64)


T, B, D, M = 4, 128, 512, 128
TEMP = 0.1
QS = 0.3
SC = 2.0
MS = SC * TEMP / (QS * np.sqrt(D))
WS = QS * np.sqrt(SC**2 / D + 0.4 / B)


def sigmoid(v):
    return 1.0 / (1.0 + np.exp(-v))


def setup_inputs():
    s = mx_kscale(D)
    return {"queries": bf(np.random.standard_normal((T, B, D)) * QS / s),
            "memory_items": bf(np.random.standard_normal((M, D)) * MS * s),
            "wq": bf(np.random.standard_normal((M, D)) * WS * s),
            "U_w": bf(np.random.standard_normal((D, D)) / (MS * np.sqrt(D)) / s[None, :]),
            "W_w": bf(np.random.standard_normal((D, D)) / (WS * np.sqrt(D)) / s[None, :])}


def reference(queries, memory_items, wq, U_w, W_w):
    q = f64(queries).reshape(T * B, D)
    mem = f64(memory_items)
    w = f64(wq)
    gate = sigmoid((mxq(mem, 1, "e4m3") @ mxq(f64(U_w), 1, "e4m3").T) + (mxq(w, 1, "e4m3") @ mxq(f64(W_w), 1, "e4m3").T))
    m_new = (1.0 - gate) * mem + gate * w
    logits = (mxq(q, 1, "e4m3") @ mxq(m_new, 1, "e4m3").T) / TEMP
    e = np.exp(logits - logits.max(-1, keepdims=True))
    w_att = e / e.sum(-1, keepdims=True)
    return m_new, w_att.reshape(T, B, M)

@@ -1,0 +1,211 @@
+from contextlib import ExitStack
+
+import concourse.mybir as mybir
+from concourse.masks import make_identity
+
+F32 = mybir.dt.float32
+BF16 = mybir.dt.bfloat16
+U32 = mybir.dt.uint32
+U8 = mybir.dt.uint8
+FP8X4 = mybir.dt.float8_e4m3fn_x4
+ACT = mybir.ActivationFunctionType
+ALU = mybir.AluOpType
+AXIS = mybir.AxisListType
+
+P = 128
+D = 512
+PACK = 4
+PAIR = 2 * P
+INV_TEMP = 10.0
+
+FLOPS = 2 * (2 * P * D * D) + 2 * (4 * P) * D * P
+
+
+def tile_gatedmemorymodule_pb_s_kernel(
+    tc, queries, memory_items, wq, U_w, W_w, out_0, out_1
+):
+    nc = tc.nc
+    with ExitStack() as ctx:
+        ctx.enter_context(tc.manual_schedule())
+        keep = ctx.enter_context(tc.tile_pool(name="keep", bufs=1))
+        stage = ctx.enter_context(tc.tile_pool(name="stage", bufs=3))
+        flip_psum = ctx.enter_context(tc.psum_pool(name="flip_psum", bufs=4))
+        acc_psum = ctx.enter_context(tc.psum_pool(name="acc_psum", bufs=1))
+
+        identity = keep.tile([P, P], F32)
+        make_identity(nc, identity[:])
+
+        zero = keep.tile([P, 1], F32)
+        nc.vector.memset(zero[:], 0.0)
+        warm = keep.tile([P, 1], F32)
+        nc.scalar.activation(out=warm[:], in_=zero[:], func=ACT.Exp)
+
+        slots_sb = keep.tile([P, 2 * D], BF16)
+        nc.sync.dma_start(out=slots_sb[:, 0:D], in_=memory_items)
+        nc.sync.dma_start(out=slots_sb[:, D : 2 * D], in_=wq)
+        u_rows = U_w.rearrange("(u p e) d -> u p (e d)", u=2, e=2)
+        w_rows = W_w.rearrange("(u p e) d -> u p (e d)", u=2, e=2)
+        u_sb = keep.tile([P, 2, 2 * D], BF16)
+        w_sb = keep.tile([P, 2, 2 * D], BF16)
+        for u in range(2):
+            nc.sync.dma_start(out=u_sb[:, u, :], in_=u_rows[u])
+            nc.sync.dma_start(out=w_sb[:, u, :], in_=w_rows[u])
+        q_rows = queries.rearrange("t b d -> (t b) d").rearrange("(r h j) d -> h r (j d)", h=2, j=2)
+        q_sb = keep.tile([P, 2, 2 * D], BF16)
+        for h in range(2):
+            nc.sync.dma_start(out=q_sb[:, h, :], in_=q_rows[h])
+
+        def transpose_and_quantise(rows_sb, grouped, codes, scales):
+            words = rows_sb.bitcast(F32)
+            flipped = flip_psum.tile([P, 2, PAIR], F32)
+            for j in range(2):
+                for u in range(2):
+                    first = (2 * j + u) * P
+                    nc.tensor.transpose(
+                        flipped[:, u, j * P : (j + 1) * P], words[:, first : first + P], identity[:]
+                    )
+            nc.scalar.copy(
+                out=grouped.rearrange("p c t -> p (c t)").bitcast(F32).rearrange("p (c u) -> p c u", u=2),
+                in_=flipped[:].rearrange("p u c -> p c u"),
+            )
+            nc.vector.quantize_mx(
+                out=codes.bitcast(FP8X4), scales=scales, in_=grouped.rearrange("p c t -> p (c t)")
+            )
+
+        slots_grouped = keep.tile([P, PAIR, PACK], BF16, align_bytes=64)
+        slot_codes = keep.tile([P, PAIR], U32, align_bytes=64)
+        slot_scales = keep.tile([P, PAIR], U8, align_bytes=64)
+        u_codes = keep.tile([P, 2 * PAIR], U32, align_bytes=64)
+        u_scales = keep.tile([P, 2 * PAIR], U8, align_bytes=64)
+        w_codes = keep.tile([P, 2 * PAIR], U32, align_bytes=64)
+        w_scales = keep.tile([P, 2 * PAIR], U8, align_bytes=64)
+        q_codes = keep.tile([P, 2 * PAIR], U32, align_bytes=64)
+        q_scales = keep.tile([P, 2 * PAIR], U8, align_bytes=64)
+
+        transpose_and_quantise(slots_sb[:], slots_grouped[:], slot_codes[:], slot_scales[:])
+        mem_grouped = slots_grouped[:, 0:P, :]
+        wq_grouped = slots_grouped[:, P:PAIR, :]
+        diff = keep.tile([P, P, PACK], F32)
+        nc.vector.tensor_tensor(out=diff[:], in0=wq_grouped, in1=mem_grouped, op=ALU.subtract)
+
+        for half in range(2):
+            cols = slice(half * PAIR, (half + 1) * PAIR)
+            for rows, codes, scales in ((u_sb, u_codes, u_scales), (w_sb, w_codes, w_scales)):
+                grouped = stage.tile([P, PAIR, PACK], BF16, align_bytes=64)
+                transpose_and_quantise(rows[:, half, :], grouped[:], codes[:, cols], scales[:, cols])
+        for half in range(2):
+            cols = slice(half * PAIR, (half + 1) * PAIR)
+            grouped = stage.tile([P, PAIR, PACK], BF16, align_bytes=64)
+            transpose_and_quantise(q_sb[:, half, :], grouped[:], q_codes[:, cols], q_scales[:, cols])
+
+        gate_ps = acc_psum.tile([P, PACK, P], F32)
+        for t in range(PACK):
+            chunk = slice(t * P, (t + 1) * P)
+            nc.tensor.matmul_mx(
+                out=gate_ps[:, t, :],
+                lhsT=u_codes[:, chunk].bitcast(FP8X4),
+                lhsT_scale=u_scales[:, chunk],
+                rhs=slot_codes[:, 0:P].bitcast(FP8X4),
+                rhs_scale=slot_scales[:, 0:P],
+                start=True,
+                stop=False,
+            )
+            nc.tensor.matmul_mx(
+                out=gate_ps[:, t, :],
+                lhsT=w_codes[:, chunk].bitcast(FP8X4),
+                lhsT_scale=w_scales[:, chunk],
+                rhs=slot_codes[:, P:PAIR].bitcast(FP8X4),
+                rhs_scale=slot_scales[:, P:PAIR],
+                start=False,
+                stop=True,
+            )
+
+        tanh_half = keep.tile([P, P, PACK], F32)
+        nc.scalar.activation(
+            out=tanh_half[:], in_=gate_ps[:].rearrange("p t m -> p m t"), func=ACT.Tanh, scale=0.5
+        )
+        step = keep.tile([P, P, PACK], F32)
+        nc.vector.scalar_tensor_tensor(
+            out=step[:].rearrange("p m t -> p (m t)"),
+            in0=tanh_half[:].rearrange("p m t -> p (m t)"),
+            scalar=1.0,
+            in1=diff[:].rearrange("p m t -> p (m t)"),
+            op0=ALU.add,
+            op1=ALU.mult,
+        )
+        mnew_grouped = keep.tile([P, P, PACK], BF16, align_bytes=64)
+        nc.vector.scalar_tensor_tensor(
+            out=mnew_grouped[:].rearrange("p m t -> p (m t)"),
+            in0=step[:].rearrange("p m t -> p (m t)"),
+            scalar=0.5,
+            in1=mem_grouped.rearrange("p m t -> p (m t)"),
+            op0=ALU.mult,
+            op1=ALU.add,
+        )
+        mnew_codes = keep.tile([P, P], U32, align_bytes=64)
+        mnew_scales = keep.tile([P, P], U8, align_bytes=64)
+        nc.vector.quantize_mx(
+            out=mnew_codes[:].bitcast(FP8X4),
+            scales=mnew_scales[:],
+            in_=mnew_grouped[:].rearrange("p m t -> p (m t)"),
+        )
+        mnew_planes = keep.tile([P, PACK, P], F32)
+        nc.vector.scalar_tensor_tensor(
+            out=mnew_planes[:],
+            in0=step[:].rearrange("p m t -> p t m"),
+            scalar=0.5,
+            in1=mem_grouped.rearrange("p m t -> p t m"),
+            op0=ALU.mult,
+            op1=ALU.add,
+        )
+
+        logit_ps = acc_psum.tile([P, PACK, P], F32)
+        for j in range(PACK):
+            chunk = slice(j * P, (j + 1) * P)
+            nc.tensor.matmul_mx(
+                out=logit_ps[:, j, :],
+                lhsT=q_codes[:, chunk].bitcast(FP8X4),
+                lhsT_scale=q_scales[:, chunk],
+                rhs=mnew_codes[:].bitcast(FP8X4),
+                rhs_scale=mnew_scales[:],
+                start=True,
+                stop=True,
+            )
+        back_ps = acc_psum.tile([P, PACK, P], F32)
+        for t in range(PACK):
+            nc.tensor.transpose(back_ps[:, t, :], mnew_planes[:, t, :], identity[:])
+
+        top = keep.tile([P, PACK], F32)
+        nc.vector.reduce_max(out=top[:], in_=logit_ps[:], axis=AXIS.X)
+        shift = keep.tile([P, PACK], F32)
+        nc.vector.tensor_scalar_mul(out=shift[:], in0=top[:], scalar1=-INV_TEMP)
+        expd = keep.tile([P, PACK, P], F32)
+        sums = keep.tile([P, PACK], F32)
+        for j in range(PACK):
+            nc.scalar.activation(
+                out=expd[:, j, :],
+                in_=logit_ps[:, j, :],
+                func=ACT.Exp,
+                bias=shift[:, j : j + 1],
+                scale=INV_TEMP,
+                accum_out=sums[:, j : j + 1],
+            )
+        mnew_out = keep.tile([P, D], F32)
+        nc.vector.tensor_copy(
+            out=mnew_out[:].rearrange("m (u p e) -> m u p e", u=2, e=2),
+            in_=back_ps[:].rearrange("m (u e) p -> m u p e", u=2),
+        )
+        nc.sync.dma_start(out=out_0, in_=mnew_out[:])
+
+        inv_sums = keep.tile([P, PACK], F32)
+        nc.vector.reciprocal(out=inv_sums[:], in_=sums[:])
+        w_att = keep.tile([P, PACK, P], F32)
+        nc.vector.tensor_tensor(
+            out=w_att[:],
+            in0=expd[:],
+            in1=inv_sums[:].unsqueeze(2).to_broadcast([P, PACK, P]),
+            op=ALU.mult,
+        )
+        nc.sync.dma_start(
+            out=out_1.rearrange("t b m -> (t b) m").rearrange("(r j) m -> r j m", j=PACK), in_=w_att[:]
+        )

@@ -29,8 +29,10 @@ def tile_gatedmemorymodule_pb_s_kernel(
         ctx.enter_context(tc.manual_schedule())
         keep = ctx.enter_context(tc.tile_pool(name="keep", bufs=1))
         stage = ctx.enter_context(tc.tile_pool(name="stage", bufs=3))
-        flip_psum = ctx.enter_context(tc.psum_pool(name="flip_psum", bufs=4))
-        acc_psum = ctx.enter_context(tc.psum_pool(name="acc_psum", bufs=1))
+        work = ctx.enter_context(tc.tile_pool(name="work", bufs=2))
+        flip_psum = ctx.enter_context(tc.psum_pool(name="flip_psum", bufs=3))
+        half_psum = ctx.enter_context(tc.psum_pool(name="half_psum", bufs=2))
+        back_psum = ctx.enter_context(tc.psum_pool(name="back_psum", bufs=1))
 
         identity = keep.tile([P, P], F32)
         make_identity(nc, identity[:])
@@ -55,7 +57,7 @@ def tile_gatedmemorymodule_pb_s_kernel(
         for h in range(2):
             nc.sync.dma_start(out=q_sb[:, h, :], in_=q_rows[h])
 
-        def transpose_and_quantise(rows_sb, grouped, codes, scales):
+        def transpose_pair(rows_sb, grouped):
             words = rows_sb.bitcast(F32)
             flipped = flip_psum.tile([P, 2, PAIR], F32)
             for j in range(2):
@@ -68,6 +70,8 @@ def tile_gatedmemorymodule_pb_s_kernel(
                 out=grouped.rearrange("p c t -> p (c t)").bitcast(F32).rearrange("p (c u) -> p c u", u=2),
                 in_=flipped[:].rearrange("p u c -> p c u"),
             )
+
+        def quantise(grouped, codes, scales):
             nc.vector.quantize_mx(
                 out=codes.bitcast(FP8X4), scales=scales, in_=grouped.rearrange("p c t -> p (c t)")
             )
@@ -82,130 +86,140 @@ def tile_gatedmemorymodule_pb_s_kernel(
         q_codes = keep.tile([P, 2 * PAIR], U32, align_bytes=64)
         q_scales = keep.tile([P, 2 * PAIR], U8, align_bytes=64)
 
-        transpose_and_quantise(slots_sb[:], slots_grouped[:], slot_codes[:], slot_scales[:])
-        mem_grouped = slots_grouped[:, 0:P, :]
-        wq_grouped = slots_grouped[:, P:PAIR, :]
-        diff = keep.tile([P, P, PACK], F32)
-        nc.vector.tensor_tensor(out=diff[:], in0=wq_grouped, in1=mem_grouped, op=ALU.subtract)
+        transpose_pair(slots_sb[:], slots_grouped[:])
+        quantise(slots_grouped[:], slot_codes[:], slot_scales[:])
+        mem_planes = slots_grouped[:, 0:P, :].rearrange("p m t -> p t m")
+        wq_planes = slots_grouped[:, P:PAIR, :].rearrange("p m t -> p t m")
+        diff_planes = keep.tile([P, PACK, P], F32)
+        nc.vector.tensor_tensor(out=diff_planes[:], in0=wq_planes, in1=mem_planes, op=ALU.subtract)
 
-        for half in range(2):
-            cols = slice(half * PAIR, (half + 1) * PAIR)
+        for u in range(2):
+            cols = slice(u * PAIR, (u + 1) * PAIR)
             for rows, codes, scales in ((u_sb, u_codes, u_scales), (w_sb, w_codes, w_scales)):
                 grouped = stage.tile([P, PAIR, PACK], BF16, align_bytes=64)
-                transpose_and_quantise(rows[:, half, :], grouped[:], codes[:, cols], scales[:, cols])
-        for half in range(2):
-            cols = slice(half * PAIR, (half + 1) * PAIR)
-            grouped = stage.tile([P, PAIR, PACK], BF16, align_bytes=64)
-            transpose_and_quantise(q_sb[:, half, :], grouped[:], q_codes[:, cols], q_scales[:, cols])
+                transpose_pair(rows[:, u, :], grouped[:])
+                quantise(grouped[:], codes[:, cols], scales[:, cols])
 
-        gate_ps = acc_psum.tile([P, PACK, P], F32)
-        for t in range(PACK):
-            chunk = slice(t * P, (t + 1) * P)
-            nc.tensor.matmul_mx(
-                out=gate_ps[:, t, :],
-                lhsT=u_codes[:, chunk].bitcast(FP8X4),
-                lhsT_scale=u_scales[:, chunk],
-                rhs=slot_codes[:, 0:P].bitcast(FP8X4),
-                rhs_scale=slot_scales[:, 0:P],
-                start=True,
-                stop=False,
-            )
-            nc.tensor.matmul_mx(
-                out=gate_ps[:, t, :],
-                lhsT=w_codes[:, chunk].bitcast(FP8X4),
-                lhsT_scale=w_scales[:, chunk],
-                rhs=slot_codes[:, P:PAIR].bitcast(FP8X4),
-                rhs_scale=slot_scales[:, P:PAIR],
-                start=False,
-                stop=True,
-            )
+        gate_halves = []
+        for u in range(2):
+            gate_ps = half_psum.tile([P, 2, P], F32)
+            gate_halves.append(gate_ps)
+            for e in range(2):
+                chunk = slice((2 * u + e) * P, (2 * u + e + 1) * P)
+                nc.tensor.matmul_mx(
+                    out=gate_ps[:, e, :],
+                    lhsT=u_codes[:, chunk].bitcast(FP8X4),
+                    lhsT_scale=u_scales[:, chunk],
+                    rhs=slot_codes[:, 0:P].bitcast(FP8X4),
+                    rhs_scale=slot_scales[:, 0:P],
+                    start=True,
+                    stop=False,
+                )
+                nc.tensor.matmul_mx(
+                    out=gate_ps[:, e, :],
+                    lhsT=w_codes[:, chunk].bitcast(FP8X4),
+                    lhsT_scale=w_scales[:, chunk],
+                    rhs=slot_codes[:, P:PAIR].bitcast(FP8X4),
+                    rhs_scale=slot_scales[:, P:PAIR],
+                    start=False,
+                    stop=True,
+                )
 
-        tanh_half = keep.tile([P, P, PACK], F32)
-        nc.scalar.activation(
-            out=tanh_half[:], in_=gate_ps[:].rearrange("p t m -> p m t"), func=ACT.Tanh, scale=0.5
-        )
-        step = keep.tile([P, P, PACK], F32)
-        nc.vector.scalar_tensor_tensor(
-            out=step[:].rearrange("p m t -> p (m t)"),
-            in0=tanh_half[:].rearrange("p m t -> p (m t)"),
-            scalar=1.0,
-            in1=diff[:].rearrange("p m t -> p (m t)"),
-            op0=ALU.add,
-            op1=ALU.mult,
-        )
-        mnew_grouped = keep.tile([P, P, PACK], BF16, align_bytes=64)
-        nc.vector.scalar_tensor_tensor(
-            out=mnew_grouped[:].rearrange("p m t -> p (m t)"),
-            in0=step[:].rearrange("p m t -> p (m t)"),
-            scalar=0.5,
-            in1=mem_grouped.rearrange("p m t -> p (m t)"),
-            op0=ALU.mult,
-            op1=ALU.add,
-        )
-        mnew_codes = keep.tile([P, P], U32, align_bytes=64)
-        mnew_scales = keep.tile([P, P], U8, align_bytes=64)
-        nc.vector.quantize_mx(
-            out=mnew_codes[:].bitcast(FP8X4),
-            scales=mnew_scales[:],
-            in_=mnew_grouped[:].rearrange("p m t -> p (m t)"),
-        )
         mnew_planes = keep.tile([P, PACK, P], F32)
-        nc.vector.scalar_tensor_tensor(
-            out=mnew_planes[:],
-            in0=step[:].rearrange("p m t -> p t m"),
-            scalar=0.5,
-            in1=mem_grouped.rearrange("p m t -> p t m"),
-            op0=ALU.mult,
-            op1=ALU.add,
-        )
-
-        logit_ps = acc_psum.tile([P, PACK, P], F32)
-        for j in range(PACK):
-            chunk = slice(j * P, (j + 1) * P)
-            nc.tensor.matmul_mx(
-                out=logit_ps[:, j, :],
-                lhsT=q_codes[:, chunk].bitcast(FP8X4),
-                lhsT_scale=q_scales[:, chunk],
-                rhs=mnew_codes[:].bitcast(FP8X4),
-                rhs_scale=mnew_scales[:],
-                start=True,
-                stop=True,
+        mnew_grouped = keep.tile([P, P, PACK], BF16, align_bytes=64)
+        for u in range(2):
+            ts = slice(2 * u, 2 * u + 2)
+            tanh_half = work.tile([P, 2, P], F32)
+            nc.scalar.activation(out=tanh_half[:], in_=gate_halves[u][:], func=ACT.Tanh, scale=0.5)
+            step = work.tile([P, 2, P], F32)
+            nc.vector.scalar_tensor_tensor(
+                out=step[:],
+                in0=tanh_half[:],
+                scalar=1.0,
+                in1=diff_planes[:, ts, :],
+                op0=ALU.add,
+                op1=ALU.mult,
             )
-        back_ps = acc_psum.tile([P, PACK, P], F32)
+            nc.vector.scalar_tensor_tensor(
+                out=mnew_planes[:, ts, :],
+                in0=step[:],
+                scalar=0.5,
+                in1=mem_planes[:, ts, :],
+                op0=ALU.mult,
+                op1=ALU.add,
+            )
+            nc.vector.tensor_copy(
+                out=mnew_grouped[:, :, ts], in_=mnew_planes[:, ts, :].rearrange("p e m -> p m e")
+            )
+
+        q_grouped = []
+        for h in range(2):
+            grouped = stage.tile([P, PAIR, PACK], BF16, align_bytes=64)
+            q_grouped.append(grouped)
+            transpose_pair(q_sb[:, h, :], grouped[:])
+
+        back_ps = back_psum.tile([P, PACK, P], F32)
         for t in range(PACK):
             nc.tensor.transpose(back_ps[:, t, :], mnew_planes[:, t, :], identity[:])
-
-        top = keep.tile([P, PACK], F32)
-        nc.vector.reduce_max(out=top[:], in_=logit_ps[:], axis=AXIS.X)
-        shift = keep.tile([P, PACK], F32)
-        nc.vector.tensor_scalar_mul(out=shift[:], in0=top[:], scalar1=-INV_TEMP)
-        expd = keep.tile([P, PACK, P], F32)
-        sums = keep.tile([P, PACK], F32)
-        for j in range(PACK):
-            nc.scalar.activation(
-                out=expd[:, j, :],
-                in_=logit_ps[:, j, :],
-                func=ACT.Exp,
-                bias=shift[:, j : j + 1],
-                scale=INV_TEMP,
-                accum_out=sums[:, j : j + 1],
-            )
         mnew_out = keep.tile([P, D], F32)
-        nc.vector.tensor_copy(
+        nc.scalar.copy(
             out=mnew_out[:].rearrange("m (u p e) -> m u p e", u=2, e=2),
             in_=back_ps[:].rearrange("m (u e) p -> m u p e", u=2),
         )
         nc.sync.dma_start(out=out_0, in_=mnew_out[:])
 
+        mnew_codes = keep.tile([P, P], U32, align_bytes=64)
+        mnew_scales = keep.tile([P, P], U8, align_bytes=64)
+        quantise(mnew_grouped[:], mnew_codes[:], mnew_scales[:])
+        for h in range(2):
+            cols = slice(h * PAIR, (h + 1) * PAIR)
+            quantise(q_grouped[h][:], q_codes[:, cols], q_scales[:, cols])
+
+        logit_halves = []
+        for h in range(2):
+            logit_ps = half_psum.tile([P, 2, P], F32)
+            logit_halves.append(logit_ps)
+            for i in range(2):
+                chunk = slice((2 * h + i) * P, (2 * h + i + 1) * P)
+                nc.tensor.matmul_mx(
+                    out=logit_ps[:, i, :],
+                    lhsT=q_codes[:, chunk].bitcast(FP8X4),
+                    lhsT_scale=q_scales[:, chunk],
+                    rhs=mnew_codes[:].bitcast(FP8X4),
+                    rhs_scale=mnew_scales[:],
+                    start=True,
+                    stop=True,
+                )
+
+        negated = keep.tile([P, PACK, P], F32)
+        shift = keep.tile([P, PACK], F32)
+        expd = keep.tile([P, PACK, P], F32)
+        sums = keep.tile([P, PACK], F32)
         inv_sums = keep.tile([P, PACK], F32)
-        nc.vector.reciprocal(out=inv_sums[:], in_=sums[:])
         w_att = keep.tile([P, PACK, P], F32)
-        nc.vector.tensor_tensor(
-            out=w_att[:],
-            in0=expd[:],
-            in1=inv_sums[:].unsqueeze(2).to_broadcast([P, PACK, P]),
-            op=ALU.mult,
-        )
-        nc.sync.dma_start(
-            out=out_1.rearrange("t b m -> (t b) m").rearrange("(r j) m -> r j m", j=PACK), in_=w_att[:]
-        )
+        for j in range(PACK):
+            nc.vector.tensor_scalar(
+                out=negated[:, j, :],
+                in0=logit_halves[j // 2][:, j % 2, :],
+                scalar1=-INV_TEMP,
+                scalar2=None,
+                op0=ALU.mult,
+                op1=ALU.min,
+                accum_out=shift[:, j : j + 1],
+            )
+            nc.scalar.activation(
+                out=expd[:, j, :],
+                in_=negated[:, j, :],
+                func=ACT.Exp,
+                bias=shift[:, j : j + 1],
+                scale=-1.0,
+                accum_out=sums[:, j : j + 1],
+            )
+        out_rows = out_1.rearrange("t b m -> (t b) m").rearrange("(r j) m -> r j m", j=PACK)
+        for h in range(2):
+            for j in (2 * h, 2 * h + 1):
+                nc.vector.reciprocal(out=inv_sums[:, j : j + 1], in_=sums[:, j : j + 1])
+                nc.vector.tensor_scalar_mul(
+                    out=w_att[:, j, :], in0=expd[:, j, :], scalar1=inv_sums[:, j : j + 1]
+                )
+            nc.sync.dma_start(out=out_rows[:, 2 * h : 2 * h + 2, :], in_=w_att[:, 2 * h : 2 * h + 2, :])

@@ -16,6 +16,7 @@ P = 128
 D = 512
 PACK = 4
 PAIR = 2 * P
+WARM_PASSES = 16
 INV_TEMP = 10.0
 
 FLOPS = 2 * (2 * P * D * D) + 2 * (4 * P) * D * P
@@ -41,6 +42,23 @@ def tile_gatedmemorymodule_pb_s_kernel(
         nc.vector.memset(zero[:], 0.0)
         warm = keep.tile([P, 1], F32)
         nc.scalar.activation(out=warm[:], in_=zero[:], func=ACT.Exp)
+
+        idle_values = keep.tile([P, P * PACK], BF16, align_bytes=64)
+        idle_codes = keep.tile([P, P], U32, align_bytes=64)
+        idle_scales = keep.tile([P, P], U8, align_bytes=64)
+        nc.vector.memset(idle_values[:], 0.0)
+        nc.vector.quantize_mx(out=idle_codes[:].bitcast(FP8X4), scales=idle_scales[:], in_=idle_values[:])
+        idle_ps = back_psum.tile([P, PACK, P], F32, tag="back_ps")
+        for i in range(WARM_PASSES):
+            nc.tensor.matmul_mx(
+                out=idle_ps[:, i % PACK, :],
+                lhsT=idle_codes[:].bitcast(FP8X4),
+                lhsT_scale=idle_scales[:],
+                rhs=idle_codes[:].bitcast(FP8X4),
+                rhs_scale=idle_scales[:],
+                start=True,
+                stop=True,
+            )
 
         slots_sb = keep.tile([P, 2 * D], BF16)
         nc.sync.dma_start(out=slots_sb[:, 0:D], in_=memory_items)

@@ -15,8 +15,6 @@ AXIS = mybir.AxisListType
 P = 128
 D = 512
 PACK = 4
-PAIR = 2 * P
-WARM_PASSES = 16
 INV_TEMP = 10.0
 
 FLOPS = 2 * (2 * P * D * D) + 2 * (4 * P) * D * P
@@ -29,9 +27,8 @@ def tile_gatedmemorymodule_pb_s_kernel(
     with ExitStack() as ctx:
         ctx.enter_context(tc.manual_schedule())
         keep = ctx.enter_context(tc.tile_pool(name="keep", bufs=1))
-        stage = ctx.enter_context(tc.tile_pool(name="stage", bufs=3))
-        work = ctx.enter_context(tc.tile_pool(name="work", bufs=2))
-        flip_psum = ctx.enter_context(tc.psum_pool(name="flip_psum", bufs=3))
+        stage = ctx.enter_context(tc.tile_pool(name="stage", bufs=4))
+        flip_psum = ctx.enter_context(tc.psum_pool(name="flip_psum", bufs=4))
         half_psum = ctx.enter_context(tc.psum_pool(name="half_psum", bufs=2))
         back_psum = ctx.enter_context(tc.psum_pool(name="back_psum", bufs=1))
 
@@ -43,84 +40,68 @@ def tile_gatedmemorymodule_pb_s_kernel(
         warm = keep.tile([P, 1], F32)
         nc.scalar.activation(out=warm[:], in_=zero[:], func=ACT.Exp)
 
-        idle_values = keep.tile([P, P * PACK], BF16, align_bytes=64)
-        idle_codes = keep.tile([P, P], U32, align_bytes=64)
-        idle_scales = keep.tile([P, P], U8, align_bytes=64)
-        nc.vector.memset(idle_values[:], 0.0)
-        nc.vector.quantize_mx(out=idle_codes[:].bitcast(FP8X4), scales=idle_scales[:], in_=idle_values[:])
-        idle_ps = back_psum.tile([P, PACK, P], F32, tag="back_ps")
-        for i in range(WARM_PASSES):
-            nc.tensor.matmul_mx(
-                out=idle_ps[:, i % PACK, :],
-                lhsT=idle_codes[:].bitcast(FP8X4),
-                lhsT_scale=idle_scales[:],
-                rhs=idle_codes[:].bitcast(FP8X4),
-                rhs_scale=idle_scales[:],
-                start=True,
-                stop=True,
-            )
-
-        slots_sb = keep.tile([P, 2 * D], BF16)
-        nc.sync.dma_start(out=slots_sb[:, 0:D], in_=memory_items)
-        nc.sync.dma_start(out=slots_sb[:, D : 2 * D], in_=wq)
+        slots_sb = keep.tile([P, 2, D], BF16)
+        nc.sync.dma_start(out=slots_sb[:, 0, :], in_=memory_items)
+        nc.sync.dma_start(out=slots_sb[:, 1, :], in_=wq)
         u_rows = U_w.rearrange("(u p e) d -> u p (e d)", u=2, e=2)
         w_rows = W_w.rearrange("(u p e) d -> u p (e d)", u=2, e=2)
-        u_sb = keep.tile([P, 2, 2 * D], BF16)
-        w_sb = keep.tile([P, 2, 2 * D], BF16)
+        u_sb = keep.tile([P, PACK, D], BF16)
+        w_sb = keep.tile([P, PACK, D], BF16)
         for u in range(2):
-            nc.sync.dma_start(out=u_sb[:, u, :], in_=u_rows[u])
-            nc.sync.dma_start(out=w_sb[:, u, :], in_=w_rows[u])
-        q_rows = queries.rearrange("t b d -> (t b) d").rearrange("(r h j) d -> h r (j d)", h=2, j=2)
-        q_sb = keep.tile([P, 2, 2 * D], BF16)
+            ts = slice(2 * u, 2 * u + 2)
+            nc.sync.dma_start(out=u_sb[:, ts, :].rearrange("p e d -> p (e d)"), in_=u_rows[u])
+            nc.sync.dma_start(out=w_sb[:, ts, :].rearrange("p e d -> p (e d)"), in_=w_rows[u])
+        q_rows = queries.rearrange("t b d -> (t b) d").rearrange("(r h i) d -> h r (i d)", h=2, i=2)
+        q_sb = keep.tile([P, PACK, D], BF16)
         for h in range(2):
-            nc.sync.dma_start(out=q_sb[:, h, :], in_=q_rows[h])
+            js = slice(2 * h, 2 * h + 2)
+            nc.sync.dma_start(out=q_sb[:, js, :].rearrange("r i d -> r (i d)"), in_=q_rows[h])
 
-        def transpose_pair(rows_sb, grouped):
+        def transpose_tile(rows_sb, grouped):
             words = rows_sb.bitcast(F32)
-            flipped = flip_psum.tile([P, 2, PAIR], F32)
-            for j in range(2):
-                for u in range(2):
-                    first = (2 * j + u) * P
-                    nc.tensor.transpose(
-                        flipped[:, u, j * P : (j + 1) * P], words[:, first : first + P], identity[:]
-                    )
+            flipped = flip_psum.tile([P, 2, P], F32)
+            for u in range(2):
+                nc.tensor.transpose(flipped[:, u, :], words[:, u * P : (u + 1) * P], identity[:])
             nc.scalar.copy(
-                out=grouped.rearrange("p c t -> p (c t)").bitcast(F32).rearrange("p (c u) -> p c u", u=2),
-                in_=flipped[:].rearrange("p u c -> p c u"),
+                out=grouped.rearrange("p r t -> p (r t)").bitcast(F32).rearrange("p (r u) -> p r u", u=2),
+                in_=flipped[:].rearrange("p u r -> p r u"),
             )
 
         def quantise(grouped, codes, scales):
             nc.vector.quantize_mx(
-                out=codes.bitcast(FP8X4), scales=scales, in_=grouped.rearrange("p c t -> p (c t)")
+                out=codes.bitcast(FP8X4), scales=scales, in_=grouped.rearrange("p r t -> p (r t)")
             )
 
-        slots_grouped = keep.tile([P, PAIR, PACK], BF16, align_bytes=64)
-        slot_codes = keep.tile([P, PAIR], U32, align_bytes=64)
-        slot_scales = keep.tile([P, PAIR], U8, align_bytes=64)
-        u_codes = keep.tile([P, 2 * PAIR], U32, align_bytes=64)
-        u_scales = keep.tile([P, 2 * PAIR], U8, align_bytes=64)
-        w_codes = keep.tile([P, 2 * PAIR], U32, align_bytes=64)
-        w_scales = keep.tile([P, 2 * PAIR], U8, align_bytes=64)
-        q_codes = keep.tile([P, 2 * PAIR], U32, align_bytes=64)
-        q_scales = keep.tile([P, 2 * PAIR], U8, align_bytes=64)
+        slot_codes = keep.tile([P, 2 * P], U32, align_bytes=64)
+        slot_scales = keep.tile([P, 2 * P], U8, align_bytes=64)
+        u_codes = keep.tile([P, PACK * P], U32, align_bytes=64)
+        u_scales = keep.tile([P, PACK * P], U8, align_bytes=64)
+        w_codes = keep.tile([P, PACK * P], U32, align_bytes=64)
+        w_scales = keep.tile([P, PACK * P], U8, align_bytes=64)
+        q_codes = keep.tile([P, PACK * P], U32, align_bytes=64)
+        q_scales = keep.tile([P, PACK * P], U8, align_bytes=64)
 
-        transpose_pair(slots_sb[:], slots_grouped[:])
-        quantise(slots_grouped[:], slot_codes[:], slot_scales[:])
-        mem_planes = slots_grouped[:, 0:P, :].rearrange("p m t -> p t m")
-        wq_planes = slots_grouped[:, P:PAIR, :].rearrange("p m t -> p t m")
+        slots_grouped = keep.tile([P, 2, P, PACK], BF16, align_bytes=64)
+        for i in range(2):
+            chunk = slice(i * P, (i + 1) * P)
+            transpose_tile(slots_sb[:, i, :], slots_grouped[:, i, :, :])
+            quantise(slots_grouped[:, i, :, :], slot_codes[:, chunk], slot_scales[:, chunk])
+        mem_planes = slots_grouped[:, 0, :, :].rearrange("p m t -> p t m")
+        wq_planes = slots_grouped[:, 1, :, :].rearrange("p m t -> p t m")
         diff_planes = keep.tile([P, PACK, P], F32)
         nc.vector.tensor_tensor(out=diff_planes[:], in0=wq_planes, in1=mem_planes, op=ALU.subtract)
 
         for u in range(2):
-            cols = slice(u * PAIR, (u + 1) * PAIR)
             for rows, codes, scales in ((u_sb, u_codes, u_scales), (w_sb, w_codes, w_scales)):
-                grouped = stage.tile([P, PAIR, PACK], BF16, align_bytes=64)
-                transpose_pair(rows[:, u, :], grouped[:])
-                quantise(grouped[:], codes[:, cols], scales[:, cols])
+                for t in (2 * u, 2 * u + 1):
+                    chunk = slice(t * P, (t + 1) * P)
+                    grouped = stage.tile([P, P, PACK], BF16, align_bytes=64)
+                    transpose_tile(rows[:, t, :], grouped[:])
+                    quantise(grouped[:], codes[:, chunk], scales[:, chunk])
 
         gate_halves = []
         for u in range(2):
-            gate_ps = half_psum.tile([P, 2, P], F32)
+            gate_ps = half_psum.tile([P, 2, P], F32, tag="half")
             gate_halves.append(gate_ps)
             for e in range(2):
                 chunk = slice((2 * u + e) * P, (2 * u + e + 1) * P)
@@ -137,44 +118,73 @@ def tile_gatedmemorymodule_pb_s_kernel(
                     out=gate_ps[:, e, :],
                     lhsT=w_codes[:, chunk].bitcast(FP8X4),
                     lhsT_scale=w_scales[:, chunk],
-                    rhs=slot_codes[:, P:PAIR].bitcast(FP8X4),
-                    rhs_scale=slot_scales[:, P:PAIR],
+                    rhs=slot_codes[:, P : 2 * P].bitcast(FP8X4),
+                    rhs_scale=slot_scales[:, P : 2 * P],
                     start=False,
                     stop=True,
                 )
 
+        tanh_planes = keep.tile([P, PACK, P], F32)
+        for u in range(2):
+            nc.scalar.activation(
+                out=tanh_planes[:, 2 * u : 2 * u + 2, :], in_=gate_halves[u][:], func=ACT.Tanh, scale=0.5
+            )
+
+        q_grouped = []
+        for j in range(PACK):
+            grouped = stage.tile([P, P, PACK], BF16, align_bytes=64)
+            q_grouped.append(grouped)
+            transpose_tile(q_sb[:, j, :], grouped[:])
+
+        step_planes = keep.tile([P, PACK, P], F32)
         mnew_planes = keep.tile([P, PACK, P], F32)
         mnew_grouped = keep.tile([P, P, PACK], BF16, align_bytes=64)
-        for u in range(2):
+        mnew_codes = keep.tile([P, P], U32, align_bytes=64)
+        mnew_scales = keep.tile([P, P], U8, align_bytes=64)
+
+        def take_step(u):
             ts = slice(2 * u, 2 * u + 2)
-            tanh_half = work.tile([P, 2, P], F32)
-            nc.scalar.activation(out=tanh_half[:], in_=gate_halves[u][:], func=ACT.Tanh, scale=0.5)
-            step = work.tile([P, 2, P], F32)
             nc.vector.scalar_tensor_tensor(
-                out=step[:],
-                in0=tanh_half[:],
+                out=step_planes[:, ts, :],
+                in0=tanh_planes[:, ts, :],
                 scalar=1.0,
                 in1=diff_planes[:, ts, :],
                 op0=ALU.add,
                 op1=ALU.mult,
             )
+
+        def blend(u):
+            ts = slice(2 * u, 2 * u + 2)
             nc.vector.scalar_tensor_tensor(
                 out=mnew_planes[:, ts, :],
-                in0=step[:],
+                in0=step_planes[:, ts, :],
                 scalar=0.5,
                 in1=mem_planes[:, ts, :],
                 op0=ALU.mult,
                 op1=ALU.add,
             )
+
+        def round_and_group(u):
+            ts = slice(2 * u, 2 * u + 2)
             nc.vector.tensor_copy(
                 out=mnew_grouped[:, :, ts], in_=mnew_planes[:, ts, :].rearrange("p e m -> p m e")
             )
 
-        q_grouped = []
-        for h in range(2):
-            grouped = stage.tile([P, PAIR, PACK], BF16, align_bytes=64)
-            q_grouped.append(grouped)
-            transpose_pair(q_sb[:, h, :], grouped[:])
+        def quantise_queries(j):
+            chunk = slice(j * P, (j + 1) * P)
+            quantise(q_grouped[j][:], q_codes[:, chunk], q_scales[:, chunk])
+
+        take_step(0)
+        blend(0)
+        take_step(1)
+        round_and_group(0)
+        blend(1)
+        quantise_queries(0)
+        round_and_group(1)
+        quantise_queries(1)
+        quantise(mnew_grouped[:], mnew_codes[:], mnew_scales[:])
+        quantise_queries(2)
+        quantise_queries(3)
 
         back_ps = back_psum.tile([P, PACK, P], F32)
         for t in range(PACK):
@@ -186,16 +196,9 @@ def tile_gatedmemorymodule_pb_s_kernel(
         )
         nc.sync.dma_start(out=out_0, in_=mnew_out[:])
 
-        mnew_codes = keep.tile([P, P], U32, align_bytes=64)
-        mnew_scales = keep.tile([P, P], U8, align_bytes=64)
-        quantise(mnew_grouped[:], mnew_codes[:], mnew_scales[:])
-        for h in range(2):
-            cols = slice(h * PAIR, (h + 1) * PAIR)
-            quantise(q_grouped[h][:], q_codes[:, cols], q_scales[:, cols])
-
         logit_halves = []
         for h in range(2):
-            logit_ps = half_psum.tile([P, 2, P], F32)
+            logit_ps = half_psum.tile([P, 2, P], F32, tag="half")
             logit_halves.append(logit_ps)
             for i in range(2):
                 chunk = slice((2 * h + i) * P, (2 * h + i + 1) * P)
@@ -235,9 +238,10 @@ def tile_gatedmemorymodule_pb_s_kernel(
             )
         out_rows = out_1.rearrange("t b m -> (t b) m").rearrange("(r j) m -> r j m", j=PACK)
         for h in range(2):
+            js = slice(2 * h, 2 * h + 2)
+            nc.vector.reciprocal(out=inv_sums[:, js], in_=sums[:, js])
             for j in (2 * h, 2 * h + 1):
-                nc.vector.reciprocal(out=inv_sums[:, j : j + 1], in_=sums[:, j : j + 1])
                 nc.vector.tensor_scalar_mul(
                     out=w_att[:, j, :], in0=expd[:, j, :], scalar1=inv_sums[:, j : j + 1]
                 )
-            nc.sync.dma_start(out=out_rows[:, 2 * h : 2 * h + 2, :], in_=w_att[:, 2 * h : 2 * h + 2, :])
+            nc.sync.dma_start(out=out_rows[:, js, :], in_=w_att[:, js, :])

from contextlib import ExitStack

import concourse.mybir as mybir
from concourse.masks import make_identity

F32 = mybir.dt.float32
BF16 = mybir.dt.bfloat16
U32 = mybir.dt.uint32
U8 = mybir.dt.uint8
FP8X4 = mybir.dt.float8_e4m3fn_x4
ACT = mybir.ActivationFunctionType
ALU = mybir.AluOpType
AXIS = mybir.AxisListType

P = 128
D = 512
PACK = 4
INV_TEMP = 10.0

FLOPS = 2 * (2 * P * D * D) + 2 * (4 * P) * D * P


def tile_gatedmemorymodule_pb_s_kernel(
    tc, queries, memory_items, wq, U_w, W_w, out_0, out_1
):
    nc = tc.nc
    with ExitStack() as ctx:
        ctx.enter_context(tc.manual_schedule())
        keep = ctx.enter_context(tc.tile_pool(name="keep", bufs=1))
        stage = ctx.enter_context(tc.tile_pool(name="stage", bufs=4))
        flip_psum = ctx.enter_context(tc.psum_pool(name="flip_psum", bufs=4))
        half_psum = ctx.enter_context(tc.psum_pool(name="half_psum", bufs=2))
        back_psum = ctx.enter_context(tc.psum_pool(name="back_psum", bufs=1))

        identity = keep.tile([P, P], F32)
        make_identity(nc, identity[:])

        zero = keep.tile([P, 1], F32)
        nc.vector.memset(zero[:], 0.0)
        warm = keep.tile([P, 1], F32)
        nc.scalar.activation(out=warm[:], in_=zero[:], func=ACT.Exp)

        slots_sb = keep.tile([P, 2, D], BF16)
        nc.sync.dma_start(out=slots_sb[:, 0, :], in_=memory_items)
        nc.sync.dma_start(out=slots_sb[:, 1, :], in_=wq)
        u_rows = U_w.rearrange("(u p e) d -> u p (e d)", u=2, e=2)
        w_rows = W_w.rearrange("(u p e) d -> u p (e d)", u=2, e=2)
        u_sb = keep.tile([P, PACK, D], BF16)
        w_sb = keep.tile([P, PACK, D], BF16)
        for u in range(2):
            ts = slice(2 * u, 2 * u + 2)
            nc.sync.dma_start(out=u_sb[:, ts, :].rearrange("p e d -> p (e d)"), in_=u_rows[u])
            nc.sync.dma_start(out=w_sb[:, ts, :].rearrange("p e d -> p (e d)"), in_=w_rows[u])
        q_rows = queries.rearrange("t b d -> (t b) d").rearrange("(r h i) d -> h r (i d)", h=2, i=2)
        q_sb = keep.tile([P, PACK, D], BF16)
        for h in range(2):
            js = slice(2 * h, 2 * h + 2)
            nc.sync.dma_start(out=q_sb[:, js, :].rearrange("r i d -> r (i d)"), in_=q_rows[h])

        def transpose_tile(rows_sb, grouped):
            words = rows_sb.bitcast(F32)
            flipped = flip_psum.tile([P, 2, P], F32)
            for u in range(2):
                nc.tensor.transpose(flipped[:, u, :], words[:, u * P : (u + 1) * P], identity[:])
            nc.scalar.copy(
                out=grouped.rearrange("p r t -> p (r t)").bitcast(F32).rearrange("p (r u) -> p r u", u=2),
                in_=flipped[:].rearrange("p u r -> p r u"),
            )

        def quantise(grouped, codes, scales):
            nc.vector.quantize_mx(
                out=codes.bitcast(FP8X4), scales=scales, in_=grouped.rearrange("p r t -> p (r t)")
            )

        slot_codes = keep.tile([P, 2 * P], U32, align_bytes=64)
        slot_scales = keep.tile([P, 2 * P], U8, align_bytes=64)
        u_codes = keep.tile([P, PACK * P], U32, align_bytes=64)
        u_scales = keep.tile([P, PACK * P], U8, align_bytes=64)
        w_codes = keep.tile([P, PACK * P], U32, align_bytes=64)
        w_scales = keep.tile([P, PACK * P], U8, align_bytes=64)
        q_codes = keep.tile([P, PACK * P], U32, align_bytes=64)
        q_scales = keep.tile([P, PACK * P], U8, align_bytes=64)

        slots_grouped = keep.tile([P, 2, P, PACK], BF16, align_bytes=64)
        for i in range(2):
            chunk = slice(i * P, (i + 1) * P)
            transpose_tile(slots_sb[:, i, :], slots_grouped[:, i, :, :])
            quantise(slots_grouped[:, i, :, :], slot_codes[:, chunk], slot_scales[:, chunk])
        mem_planes = slots_grouped[:, 0, :, :].rearrange("p m t -> p t m")
        wq_planes = slots_grouped[:, 1, :, :].rearrange("p m t -> p t m")
        diff_planes = keep.tile([P, PACK, P], F32)
        nc.vector.tensor_tensor(out=diff_planes[:], in0=wq_planes, in1=mem_planes, op=ALU.subtract)

        for u in range(2):
            for rows, codes, scales in ((u_sb, u_codes, u_scales), (w_sb, w_codes, w_scales)):
                for t in (2 * u, 2 * u + 1):
                    chunk = slice(t * P, (t + 1) * P)
                    grouped = stage.tile([P, P, PACK], BF16, align_bytes=64)
                    transpose_tile(rows[:, t, :], grouped[:])
                    quantise(grouped[:], codes[:, chunk], scales[:, chunk])

        gate_halves = []
        for u in range(2):
            gate_ps = half_psum.tile([P, 2, P], F32, tag="half")
            gate_halves.append(gate_ps)
            for e in range(2):
                chunk = slice((2 * u + e) * P, (2 * u + e + 1) * P)
                nc.tensor.matmul_mx(
                    out=gate_ps[:, e, :],
                    lhsT=u_codes[:, chunk].bitcast(FP8X4),
                    lhsT_scale=u_scales[:, chunk],
                    rhs=slot_codes[:, 0:P].bitcast(FP8X4),
                    rhs_scale=slot_scales[:, 0:P],
                    start=True,
                    stop=False,
                )
                nc.tensor.matmul_mx(
                    out=gate_ps[:, e, :],
                    lhsT=w_codes[:, chunk].bitcast(FP8X4),
                    lhsT_scale=w_scales[:, chunk],
                    rhs=slot_codes[:, P : 2 * P].bitcast(FP8X4),
                    rhs_scale=slot_scales[:, P : 2 * P],
                    start=False,
                    stop=True,
                )

        tanh_planes = keep.tile([P, PACK, P], F32)
        for u in range(2):
            nc.scalar.activation(
                out=tanh_planes[:, 2 * u : 2 * u + 2, :], in_=gate_halves[u][:], func=ACT.Tanh, scale=0.5
            )

        q_grouped = []
        for j in range(PACK):
            grouped = stage.tile([P, P, PACK], BF16, align_bytes=64)
            q_grouped.append(grouped)
            transpose_tile(q_sb[:, j, :], grouped[:])

        step_planes = keep.tile([P, PACK, P], F32)
        mnew_planes = keep.tile([P, PACK, P], F32)
        mnew_grouped = keep.tile([P, P, PACK], BF16, align_bytes=64)
        mnew_codes = keep.tile([P, P], U32, align_bytes=64)
        mnew_scales = keep.tile([P, P], U8, align_bytes=64)

        def take_step(u):
            ts = slice(2 * u, 2 * u + 2)
            nc.vector.scalar_tensor_tensor(
                out=step_planes[:, ts, :],
                in0=tanh_planes[:, ts, :],
                scalar=1.0,
                in1=diff_planes[:, ts, :],
                op0=ALU.add,
                op1=ALU.mult,
            )

        def blend(u):
            ts = slice(2 * u, 2 * u + 2)
            nc.vector.scalar_tensor_tensor(
                out=mnew_planes[:, ts, :],
                in0=step_planes[:, ts, :],
                scalar=0.5,
                in1=mem_planes[:, ts, :],
                op0=ALU.mult,
                op1=ALU.add,
            )

        def round_and_group(u):
            ts = slice(2 * u, 2 * u + 2)
            nc.vector.tensor_copy(
                out=mnew_grouped[:, :, ts], in_=mnew_planes[:, ts, :].rearrange("p e m -> p m e")
            )

        def quantise_queries(j):
            chunk = slice(j * P, (j + 1) * P)
            quantise(q_grouped[j][:], q_codes[:, chunk], q_scales[:, chunk])

        take_step(0)
        blend(0)
        take_step(1)
        round_and_group(0)
        blend(1)
        quantise_queries(0)
        round_and_group(1)
        quantise_queries(1)
        quantise(mnew_grouped[:], mnew_codes[:], mnew_scales[:])
        quantise_queries(2)
        quantise_queries(3)

        back_ps = back_psum.tile([P, PACK, P], F32)
        for t in range(PACK):
            nc.tensor.transpose(back_ps[:, t, :], mnew_planes[:, t, :], identity[:])
        mnew_out = keep.tile([P, D], F32)
        nc.scalar.copy(
            out=mnew_out[:].rearrange("m (u p e) -> m u p e", u=2, e=2),
            in_=back_ps[:].rearrange("m (u e) p -> m u p e", u=2),
        )
        nc.sync.dma_start(out=out_0, in_=mnew_out[:])

        logit_halves = []
        for h in range(2):
            logit_ps = half_psum.tile([P, 2, P], F32, tag="half")
            logit_halves.append(logit_ps)
            for i in range(2):
                chunk = slice((2 * h + i) * P, (2 * h + i + 1) * P)
                nc.tensor.matmul_mx(
                    out=logit_ps[:, i, :],
                    lhsT=q_codes[:, chunk].bitcast(FP8X4),
                    lhsT_scale=q_scales[:, chunk],
                    rhs=mnew_codes[:].bitcast(FP8X4),
                    rhs_scale=mnew_scales[:],
                    start=True,
                    stop=True,
                )

        negated = keep.tile([P, PACK, P], F32)
        shift = keep.tile([P, PACK], F32)
        expd = keep.tile([P, PACK, P], F32)
        sums = keep.tile([P, PACK], F32)
        inv_sums = keep.tile([P, PACK], F32)
        w_att = keep.tile([P, PACK, P], F32)
        for j in range(PACK):
            nc.vector.tensor_scalar(
                out=negated[:, j, :],
                in0=logit_halves[j // 2][:, j % 2, :],
                scalar1=-INV_TEMP,
                scalar2=None,
                op0=ALU.mult,
                op1=ALU.min,
                accum_out=shift[:, j : j + 1],
            )
            nc.scalar.activation(
                out=expd[:, j, :],
                in_=negated[:, j, :],
                func=ACT.Exp,
                bias=shift[:, j : j + 1],
                scale=-1.0,
                accum_out=sums[:, j : j + 1],
            )
        out_rows = out_1.rearrange("t b m -> (t b) m").rearrange("(r j) m -> r j m", j=PACK)
        for h in range(2):
            js = slice(2 * h, 2 * h + 2)
            nc.vector.reciprocal(out=inv_sums[:, js], in_=sums[:, js])
            for j in (2 * h, 2 * h + 1):
                nc.vector.tensor_scalar_mul(
                    out=w_att[:, j, :], in0=expd[:, j, :], scalar1=inv_sums[:, j : j + 1]
                )
            nc.sync.dma_start(out=out_rows[:, js, :], in_=w_att[:, js, :])
